import numpy as np
import ml_dtypes


def mxq(x, axis, fmt="e4m3"):
    dtype, down = {"e4m3": (ml_dtypes.float8_e4m3fn, 7), "e5m2": (ml_dtypes.float8_e5m2, 14)}[fmt]
    v = np.moveaxis(np.asarray(x, np.float32).astype(ml_dtypes.bfloat16).astype(np.float64), axis, -1)
    blocks = v.reshape(v.shape[:-1] + (-1, 32))
    amax = np.abs(blocks).max(-1, keepdims=True)
    byte = np.maximum(np.where(amax > 0, np.frexp(amax)[1] - 1 + 127, 0) - down, 1)
    scale = np.exp2(byte - 127.0)
    codes = (blocks / scale).astype(np.float32).astype(dtype).astype(np.float64)
    return np.moveaxis((codes * scale).reshape(v.shape), -1, axis)


WIDE = False


def mx_kscale(k):
    if not WIDE:
        return np.ones(k)
    levels = np.array([10, -10, 5, -5, 0])
    if k % 512:
        return np.exp2(np.random.permutation(np.resize(levels, k // 32))).repeat(32)
    a = np.empty((k // 512, 16))
    for p in range(k // 512):
        a[p, :8] = np.random.permutation(np.resize(levels, 8))
        for g in range(8):
            far = levels[np.abs(levels - a[p, g]) >= 10]
            a[p, g + 8] = far[np.random.randint(len(far))]
    return np.exp2(a.ravel()).repeat(32)


BF16 = ml_dtypes.bfloat16


def bf(x):
    return np.asarray(x, np.float32).astype(BF16)


def f64(x):
    return np.asarray(x).astype(np.float64)


B, RES, C, NH, RD, RW = 4, 32, 512, 8, 16, 128
N, L = B * RES, RES


def draw0():
    s, t = mx_kscale(C), mx_kscale(C)
    return {"y_h": bf(np.random.standard_normal((N, L, C)) * 0.5 * s),
            "y_w": bf(np.random.standard_normal((N, L, C)) * 0.5 * s),
            "x": bf(np.random.standard_normal((B, RES, RES, C)) * s),
            "a_logits": bf(np.random.standard_normal((B, 3 * C))),
            "Wo_h": bf(np.random.standard_normal((C, C)) * 2.0 / np.sqrt(C) * t[:, None] / s),
            "bo_h": bf(np.random.standard_normal(C) * 0.3 * t),
            "Wo_w": bf(np.random.standard_normal((C, C)) * 2.0 / np.sqrt(C) * t[:, None] / s),
            "bo_w": bf(np.random.standard_normal(C) * 0.3 * t),
            "Wmlpc": bf(np.random.standard_normal((C, C)) / np.sqrt(C) * t[:, None] / s),
            "Wp": bf(np.random.standard_normal((C, C)) * 1.5 / np.sqrt(C) / t),
            "bp": bf(np.random.standard_normal(C) * 0.3)}


def core(y_h, y_w, x, a_logits, Wo_h, bo_h, Wo_w, bo_w, Wmlpc, Wp, bp):
    h = (mxq(f64(y_h), 2, "e4m3") @ mxq(f64(Wo_h), 1, "e4m3").T) + f64(bo_h)
    h = h.reshape(B, RES, RES, C).transpose(0, 2, 1, 3)
    w = (mxq(f64(y_w), 2, "e4m3") @ mxq(f64(Wo_w), 1, "e4m3").T) + f64(bo_w)
    w = w.reshape(B, RES, RES, C)
    c = mxq(f64(x), 3, "e4m3") @ mxq(f64(Wmlpc), 1, "e4m3").T
    a = f64(a_logits).reshape(B, C, 3).transpose(2, 0, 1)
    a = np.exp(a - a.max(0, keepdims=True))
    a = (a / a.sum(0, keepdims=True))[:, :, None, None, :]
    out = h * a[0] + w * a[1] + c * a[2]
    return (mxq(out, 3, "e4m3") @ mxq(f64(Wp), 1, "e4m3").T) + f64(bp)


def e4m3fn_bytes(y):
    return np.clip(np.asarray(y, np.float64), -448.0, 448.0).astype(np.float32).astype(ml_dtypes.float8_e4m3fn).view(np.uint8)


def e4m3fn_values(b):
    return np.asarray(b, np.uint8).view(ml_dtypes.float8_e4m3fn).astype(np.float64)


def setup_inputs():
    d = draw0()
    x0 = np.asarray(d['y_w']).astype(np.float64)
    s = (np.max(np.abs(x0), axis=(0, 1), keepdims=True) / 448.0).astype(np.float32)
    out = {}
    for k, v in d.items():
        if k == 'y_w':
            out['y_w_bytes'] = e4m3fn_bytes(x0 / s.astype(np.float64))
            out['y_w_scale'] = s
        else:
            out[k] = v
    return out


def reference(y_h, y_w_bytes, y_w_scale, x, a_logits, Wo_h, bo_h, Wo_w, bo_w, Wmlpc, Wp, bp):
    return core(y_h, e4m3fn_values(y_w_bytes) * y_w_scale.astype(np.float64), x, a_logits, Wo_h, bo_h, Wo_w, bo_w, Wmlpc, Wp, bp)

@@ -1,0 +1,315 @@
+from contextlib import ExitStack
+
+import concourse.mybir as mybir
+from concourse.masks import make_identity
+
+F32 = mybir.dt.float32
+BF16 = mybir.dt.bfloat16
+U32 = mybir.dt.uint32
+U8 = mybir.dt.uint8
+FP8 = mybir.dt.float8_e4m3fn
+FP8X4 = mybir.dt.float8_e4m3fn_x4
+ALU = mybir.AluOpType
+ACT = mybir.ActivationFunctionType
+AX = mybir.AxisListType
+
+P = 128
+C = 512
+IMAGES = 4
+RES = 32
+BRANCHES = 3
+BLOCKS = 4
+G_ROWS = 16
+GROUP = G_ROWS * RES
+GROUPS = IMAGES * RES * RES // GROUP
+
+STEPS = "L0 B0 T00 E00 B1 T01 B2 M0 A0 S0 B3 N1 E01 W0 P0 T10 E10 T11 E11 N2 O2 N0 O1 M1 A1 Q0 M2 A2 S1 T20 E20 O0 T21 E21 W2 M3 A3 Q1 N3 W3 S2 Q2 S3 F O3 X04 W1"
+TAIL = "D0 D1 D2 D3 F N0 O0 X01 N1 O1 X12 N2 O2 X23 N3 O3 X34"
+LAG = 2
+HEADE = "ssssssssssss"
+
+FLOPS = 4 * 2 * (IMAGES * RES * RES) * C * C
+
+
+def tile_dynamixerblock_pb_kernel(
+    tc, y_h, y_w_bytes, y_w_scale, x, a_logits, Wo_h, bo_h, Wo_w, bo_w, Wmlpc, Wp, bp, out
+):
+    nc = tc.nc
+    with ExitStack() as ctx:
+        const = ctx.enter_context(tc.tile_pool(name="const", bufs=1))
+        raws = ctx.enter_context(tc.tile_pool(name="raws", bufs=3))
+        work = ctx.enter_context(tc.tile_pool(name="work", bufs=2))
+        ps_t = ctx.enter_context(tc.psum_pool(name="ps_t", bufs=3))
+        ps_1 = ctx.enter_context(tc.psum_pool(name="ps_1", bufs=3))
+        ps_2 = ctx.enter_context(tc.psum_pool(name="ps_2", bufs=2))
+        ctx.enter_context(tc.manual_schedule())
+
+        ident = const.tile([P, P], F32, name="ident")
+        make_identity(nc, ident[:])
+        ident_h = const.tile([P, P], F32, name="ident_h")
+        nc.vector.tensor_copy(
+            out=ident_h[:].rearrange("p (jl ih jh) -> p jl ih jh", jl=4, ih=4, jh=8),
+            in_=ident[:].rearrange("p (jh jl ih) -> p jl ih jh", jl=4, ih=4, jh=8),
+        )
+
+        def load_weight(w, pattern, name):
+            raw = raws.tile([P, BLOCKS, C], BF16, name=name, tag="wraw", bufs=4, align_bytes=64)
+            nc.sync.dma_start(out=raw[:], in_=w.rearrange(pattern, m=P))
+            return raw
+
+        def load_yh(g):
+            b, i0 = divmod(g * G_ROWS, RES)
+            raw = raws.tile([P, BLOCKS, C], BF16, name="yh_raw", tag="yh_raw", bufs=5, align_bytes=64)
+            src = y_h[b * RES : (b + 1) * RES, i0 : i0 + G_ROWS, :]
+            nc.sync.dma_start(out=raw[:], in_=src.rearrange("j (ih il) c -> j ih il c", il=BLOCKS))
+            return raw
+
+        def load_x(g):
+            b, i0 = divmod(g * G_ROWS, RES)
+            raw = raws.tile([P, BLOCKS, C], BF16, name="x_raw", tag="x_raw", bufs=5, align_bytes=64)
+            src = x[b, i0 : i0 + G_ROWS]
+            nc.sync.dma_start(out=raw[:], in_=src.rearrange("i (jh jl) c -> (i jh) jl c", jl=BLOCKS))
+            return raw
+
+        def load_yw(g):
+            raw = raws.tile([P, BLOCKS, C], U8, name="yw_raw", tag="yw_raw", bufs=5, align_bytes=64)
+            src = y_w_bytes[g * G_ROWS : (g + 1) * G_ROWS]
+            nc.sync.dma_start(out=raw[:], in_=src.rearrange("i (jh jl) c -> (i jh) jl c", jl=BLOCKS))
+            return raw
+
+        logits = const.tile([P, IMAGES, 16], BF16, name="logits")
+        nc.scalar.dma_start(out=logits[:, :, : 4 * BRANCHES], in_=a_logits.rearrange("b (p q) -> p b q", p=P))
+        bias_h = const.tile([P, BLOCKS], BF16, name="bias_h")
+        nc.scalar.dma_start(out=bias_h[:], in_=bo_h.rearrange("(p t) -> p t", p=P))
+        bias_w = const.tile([P, BLOCKS], BF16, name="bias_w")
+        nc.scalar.dma_start(out=bias_w[:], in_=bo_w.rearrange("(p t) -> p t", p=P))
+
+        wh_raw = load_weight(Wo_h, "(m t) k -> m t k", "wh_raw")
+        yh_raw = {0: load_yh(0)}
+        scale = const.tile([P, BLOCKS, C], F32, name="scale")
+        nc.sync.dma_start(out=scale[:, 0, :], in_=y_w_scale.rearrange("a o k -> (a o k)").partition_broadcast(P))
+        yw_raw = {0: load_yw(0)}
+        ww_raw = load_weight(Wo_w, "(m t) k -> m t k", "ww_raw")
+        x_raw = {0: load_x(0)}
+        wc_raw = load_weight(Wmlpc, "(m t) k -> m t k", "wc_raw")
+        yh_raw[1], x_raw[1], yw_raw[1] = load_yh(1), load_x(1), load_yw(1)
+        bp_all = const.tile([P, C], BF16, name="bp_all")
+        nc.sync.dma_start(out=bp_all[:], in_=bp.partition_broadcast(P))
+        wp_raw = load_weight(Wp, "(t m) k -> m t k", "wp_raw")
+
+        wide_all = {}
+        lg = logits[:, :, : 4 * BRANCHES].rearrange("p b (t k) -> p b t k", k=BRANCHES)
+        top = const.tile([P, IMAGES, BLOCKS], F32, name="top")
+        nc.vector.tensor_reduce(out=top[:], in_=lg, axis=AX.X, op=ALU.max)
+        wts = const.tile([P, IMAGES, BLOCKS, BRANCHES], F32, name="wts")
+        for k in range(BRANCHES):
+            nc.vector.tensor_tensor(out=wts[:, :, :, k], in0=lg[:, :, :, k], in1=top[:], op=ALU.subtract)
+        flat = wts[:].rearrange("p b t k -> p (b t k)")
+        nc.scalar.activation(out=flat, in_=flat, func=ACT.Exp)
+        total = const.tile([P, IMAGES, BLOCKS], F32, name="total")
+        nc.vector.tensor_reduce(out=total[:], in_=wts[:], axis=AX.X, op=ALU.add)
+        inv = const.tile([P, IMAGES, BLOCKS], F32, name="inv")
+        nc.vector.reciprocal(out=inv[:], in_=total[:])
+        a = const.tile([P, BRANCHES, IMAGES, BLOCKS], F32, name="a")
+        for k in range(BRANCHES):
+            nc.vector.tensor_tensor(out=a[:, k], in0=wts[:, :, :, k], in1=inv[:], op=ALU.mult)
+        bias = const.tile([P, IMAGES, BLOCKS], F32, name="bias")
+        bias_t = const.tile([P, IMAGES, BLOCKS], F32, name="bias_t")
+        for b in range(IMAGES):
+            nc.vector.tensor_tensor(out=bias[:, b], in0=a[:, 0, b], in1=bias_h[:], op=ALU.mult)
+            nc.vector.tensor_tensor(out=bias_t[:, b], in0=a[:, 1, b], in1=bias_w[:], op=ALU.mult)
+        nc.vector.tensor_tensor(out=bias[:], in0=bias[:], in1=bias_t[:], op=ALU.add)
+        for q in range(1, BLOCKS):
+            nc.vector.tensor_copy(out=scale[:, q, :], in_=scale[:, 0, :])
+
+        def turn_half(raw, idn, grouped, half):
+            words = raw[:].rearrange("p q c -> p (q c)").bitcast(F32)
+            pairs = grouped[:].bitcast(F32)
+            tr = ps_t.tile([P, 2, 2, P], F32, name="tr", tag="tr")
+            for q2 in range(2):
+                q = 2 * half + q2
+                for u in range(2):
+                    nc.tensor.transpose(tr[:, q2, u, :], words[:, 256 * q + u : 256 * (q + 1) : 2], idn[:])
+            return tr, pairs[:, 512 * half : 512 * (half + 1)]
+
+        def turn_out(tr, dst, eng):
+            o = dst.rearrange("p (q r u) -> p q r u", q=2, u=2)
+            i = tr[:].rearrange("p q u r -> p q r u")
+            if eng == "s":
+                nc.scalar.copy(out=o, in_=i)
+            else:
+                nc.vector.tensor_copy(out=o, in_=i)
+
+        def turn_pe(raw, idn, name, bufs):
+            grouped = work.tile([P, GROUP * 4], BF16, name=name + "_g", tag=name + "_g", bufs=bufs, align_bytes=64)
+            return grouped, [turn_half(raw, idn, grouped, h) for h in range(2)]
+
+        def turn(raw, idn, name, bufs, engs="ss"):
+            grouped, parts = turn_pe(raw, idn, name, bufs)
+            for (tr, dst), e in zip(parts, engs):
+                turn_out(tr, dst, e)
+            return grouped
+
+        def quantize(grouped, name, pool, bufs):
+            codes = pool.tile([P, GROUP], U32, name=name + "_c", tag=name + "_c", bufs=bufs, align_bytes=64)
+            scales = pool.tile([P, GROUP], U8, name=name + "_s", tag=name + "_s", bufs=bufs, align_bytes=64)
+            nc.vector.quantize_mx(out=codes[:].bitcast(FP8X4), scales=scales[:], in_=grouped[:])
+            return codes, scales
+
+        def widen(raw, wide, q):
+            nc.vector.tensor_tensor(out=wide[:, q : q + 1], in0=raw[:, q : q + 1].bitcast(FP8), in1=scale[:, q : q + 1], op=ALU.mult)
+
+        def mm(ps, st, sc, mv, mc):
+            nc.tensor.matmul_mx(
+                out=ps,
+                lhsT=st[0][:, sc].bitcast(FP8X4),
+                lhsT_scale=st[1][:, sc],
+                rhs=mv[0][:, mc].bitcast(FP8X4),
+                rhs_scale=mv[1][:, mc],
+                start=True,
+                stop=True,
+            )
+
+        whole = slice(0, GROUP)
+
+        def first_pe(g, t, ops):
+            sc = slice(P * t, P * (t + 1))
+            ph = ps_1.tile([P, GROUP], F32, name="ph", tag="m1")
+            mm(ph[:], wh, sc, ops["yh"], whole)
+            pc = ps_1.tile([P, GROUP], F32, name="pc", tag="m1")
+            mm(pc[:], wc, sc, ops["x"], whole)
+            pw = ps_1.tile([P, GROUP], F32, name="pw", tag="m1")
+            mm(pw[:], ww, sc, ops["yw"], whole)
+            return ph, pc, pw
+
+        def first_s(g, t, ps, sums, part):
+            b = g * G_ROWS // RES
+            ph, pc, pw = ps
+            nc.scalar.activation(
+                out=sums[:, t, :].rearrange("p (ji il jh) -> p ji il jh", ji=16, il=4),
+                in_=ph[:].rearrange("p (il ji jh) -> p ji il jh", il=4, ji=16),
+                func=ACT.Identity,
+                scale=a[:, 0, b, t : t + 1],
+                bias=bias[:, b, t : t + 1],
+            )
+            nc.scalar.activation(out=part[:, t, :], in_=pw[:], func=ACT.Identity, scale=a[:, 1, b, t : t + 1], bias=0.0)
+
+        def first_v(g, t, ps, sums):
+            b = g * G_ROWS // RES
+            nc.vector.scalar_tensor_tensor(
+                out=sums[:, t, :], in0=ps[1][:], scalar=a[:, 2, b, t : t + 1], in1=sums[:, t, :], op0=ALU.mult, op1=ALU.add
+            )
+
+        def blend_half(eng, f, sums, part, h):
+            cols = slice(128 * h, 128 * (h + 1))
+            eng.tensor_tensor(
+                out=f[:, 512 * h : 512 * (h + 1)].rearrange("p (n t) -> p n t", t=4),
+                in0=sums[:, :, cols].rearrange("p t n -> p n t"),
+                in1=part[:, :, cols].rearrange("p t n -> p n t"),
+                op=ALU.add,
+            )
+
+        def second_pe(q, fq):
+            po = ps_2.tile([P, C], F32, name="po", tag="m2")
+            mm(po[:], fq, slice(P * q, P * (q + 1)), wpq, whole)
+            return po
+
+        def second_v(po, q, res):
+            nc.vector.tensor_tensor(out=res[:, q, :], in0=po[:], in1=bp_all[:], op=ALU.add)
+
+        def second_sg(po, q, res):
+            raw = work.tile([P, C], F32, name="plain", tag="plain", bufs=2, align_bytes=64)
+            nc.scalar.copy(out=raw[:], in_=po[:])
+            nc.gpsimd.tensor_tensor(out=res[:, q, :], in0=raw[:], in1=bp_all[:], op=ALU.add)
+
+        def store(g, res, q0, q1):
+            b, i0 = divmod(g * G_ROWS, RES)
+            dst = out[b, i0 : i0 + G_ROWS].rearrange("i (jh jl) c -> (i jh) jl c", jl=BLOCKS)
+            nc.sync.dma_start(out=dst[:, q0:q1], in_=res[:, q0:q1])
+
+        def wide_tile():
+            return work.tile([P, BLOCKS, C], BF16, name="wide", tag="wide", bufs=2, align_bytes=64)
+
+        NAMES = ("yh", "x", "yw")
+        srcs = {"yh": (yh_raw, ident_h), "x": (x_raw, ident), "yw": (wide_all, ident)}
+
+        def fetch(n):
+            yh_raw[n], x_raw[n], yw_raw[n] = load_yh(n), load_x(n), load_yw(n)
+
+        for n in range(2, 5):
+            fetch(n)
+
+        wh_g = turn(wh_raw, ident, "w", 2, HEADE[0:2])
+        yh_g = turn(yh_raw[0], ident_h, "yh", 2, HEADE[2:4])
+        wh = quantize(wh_g, "wh", const, 1)
+        wide_all[0] = wide_tile()
+        ops = {0: {"yh": quantize(yh_g, "yh", work, 2)}}
+        x_g = turn(x_raw[0], ident, "x", 2, HEADE[4:6])
+        for q in range(BLOCKS):
+            widen(yw_raw[0], wide_all[0], q)
+        wc_g = turn(wc_raw, ident, "w", 2, HEADE[6:8])
+        ops[0]["x"] = quantize(x_g, "x", work, 2)
+        wc = quantize(wc_g, "wc", const, 1)
+        yw_g = turn(wide_all[0], ident, "yw", 2, HEADE[8:10])
+        ww_g = turn(ww_raw, ident, "w", 2, HEADE[10:12])
+        ops[0]["yw"] = quantize(yw_g, "yw", work, 2)
+        ww = quantize(ww_g, "ww", const, 1)
+        wide_all[1] = wide_tile()
+        for q in range(BLOCKS):
+            widen(yw_raw[1], wide_all[1], q)
+
+        fq, summed, fs, ress, pos, trs, gro, pss = {}, {}, {}, {}, {}, {}, {}, {}
+        last = GROUPS - 1
+        for g in range(GROUPS + LAG):
+            for tok in (STEPS if g < GROUPS else TAIL).split():
+                op, arg = tok[0], tok[1:]
+                i = int(arg[0]) if arg else 0
+                if op == "L" and g + 5 < GROUPS:
+                    fetch(g + 5)
+                if op in "MAS" and g < GROUPS:
+                    if g not in summed:
+                        sums = work.tile([P, BLOCKS, GROUP], F32, name="sums", tag="sums", bufs=2, align_bytes=64)
+                        part = work.tile([P, BLOCKS, GROUP], F32, name="part", tag="part", bufs=2, align_bytes=64)
+                        summed[g] = (sums, part)
+                    if op == "M":
+                        pss[i] = first_pe(g, i, ops[g])
+                    elif op == "A":
+                        first_s(g, i, pss[i], *summed[g])
+                    else:
+                        first_v(g, i, pss[i], summed[g][0])
+                if op in "TEVQ" and g + 1 < GROUPS:
+                    nm = NAMES[i]
+                    if op == "T":
+                        h = int(arg[1])
+                        if h == 0:
+                            gro[nm] = work.tile([P, GROUP * 4], BF16, name=nm + "_g", tag=nm + "_g", bufs=2, align_bytes=64)
+                        trs[arg] = turn_half(srcs[nm][0][g + 1], srcs[nm][1], gro[nm], h)
+                    elif op == "E":
+                        turn_out(*trs[arg], "s")
+                    elif op == "V":
+                        turn_out(*trs[arg], "v")
+                    else:
+                        ops.setdefault(g + 1, {})[nm] = quantize(gro[nm], nm, work, 2)
+                if op == "P" and g == 0:
+                    wp_g = turn(wp_raw, ident, "w", 2)
+                    wpq = quantize(wp_g, "wpq", const, 1)
+                if op == "W" and g + 2 < GROUPS:
+                    if i == 0:
+                        wide_all[g + 2] = wide_tile()
+                    widen(yw_raw[g + 2], wide_all[g + 2], i)
+                if op in "BD" and 0 <= g - 1 < GROUPS:
+                    if g - 1 not in fs:
+                        fs[g - 1] = work.tile([P, GROUP * 4], BF16, name="f", tag="f", bufs=2, align_bytes=64)
+                    blend_half(nc.gpsimd if op == "B" else nc.vector, fs[g - 1], *summed[g - 1], i)
+                if op == "F" and 0 <= g - 1 < GROUPS:
+                    fq[g - 1] = quantize(fs[g - 1], "f", work, 2)
+                n = g - LAG
+                if op in "NOUX" and 0 <= n:
+                    if op == "N":
+                        pos[i] = second_pe(i, fq[n])
+                    elif op == "X":
+                        store(n, ress[n], int(arg[0]), int(arg[1]))
+                    else:
+                        if n not in ress:
+                            ress[n] = work.tile([P, BLOCKS, C], F32, name="res", tag="res", bufs=2, align_bytes=64)
+                        (second_v if op == "O" else second_sg)(pos[i], i, ress[n])

@@ -23,10 +23,13 @@ G_ROWS = 16
 GROUP = G_ROWS * RES
 GROUPS = IMAGES * RES * RES // GROUP
 
-STEPS = "L0 B0 T00 E00 B1 T01 B2 M0 A0 S0 B3 N1 E01 W0 P0 T10 E10 T11 E11 N2 O2 N0 O1 M1 A1 Q0 M2 A2 S1 T20 E20 O0 T21 E21 W2 M3 A3 Q1 N3 W3 S2 Q2 S3 F O3 X04 W1"
-TAIL = "D0 D1 D2 D3 F N0 O0 X01 N1 O1 X12 N2 O2 X23 N3 O3 X34"
-LAG = 2
-HEADE = "ssssssssssss"
+MODE = "i"
+TAIL_V = True
+RING = 2
+NB = 4
+NF = 2
+ON_V = "eh0 eh1 ec0 ec1 ew0 ew1 ep0 ep1".split()
+STEPS = "C0@0 th1@0 Ah2@2 th0@0 C1@0 Sc2@2 eh0@0 tc0@0 Ah0@1 ep0@2 Th0@0 eh1@0 Sc3@2 Eh0@0 qh@0 Mw1@2 Aw1@2 qp@3 Mw2@2 ec0@0 Aw2@2 F1@3 Th1@0 Eh1@0 F0@3 Tx0@0 Qw@1 Mw3@2 tw1@0 Qx@1 N0@3 Aw3@2 tw0@0 ew1@0 O3@4 Ex0@0 Mh1@1 ew0@0 Qh@0 B3@2 Mw0@1 Ah1@1 O0@3 qw@0 Aw0@1 Mc1@1 N1@3 tp1@2 Tx1@0 O1@3 ep1@2 Sc1@1 Mh3@1 B1@2 Ex1@0 tc1@0 Mc0@1 Ah3@1 ec1@0 Tw0@0 Sc0@1 N2@3 Ew0@0 Tw1@0 Mh2@1 Ew1@0 O2@3 N3@3 qc@0 Mc2@1 B2@2 Mh0@0 B0@2 Mc3@1 tp0@1"
 
 FLOPS = 4 * 2 * (IMAGES * RES * RES) * C * C
 
@@ -39,8 +42,8 @@ def tile_dynamixerblock_pb_kernel(
         const = ctx.enter_context(tc.tile_pool(name="const", bufs=1))
         raws = ctx.enter_context(tc.tile_pool(name="raws", bufs=3))
         work = ctx.enter_context(tc.tile_pool(name="work", bufs=2))
-        ps_t = ctx.enter_context(tc.psum_pool(name="ps_t", bufs=3))
-        ps_1 = ctx.enter_context(tc.psum_pool(name="ps_1", bufs=3))
+        ps_t = ctx.enter_context(tc.psum_pool(name="ps_t", bufs=2))
+        ps_1 = ctx.enter_context(tc.psum_pool(name="ps_1", bufs=4))
         ps_2 = ctx.enter_context(tc.psum_pool(name="ps_2", bufs=2))
         ctx.enter_context(tc.manual_schedule())
 
@@ -57,25 +60,19 @@ def tile_dynamixerblock_pb_kernel(
             nc.sync.dma_start(out=raw[:], in_=w.rearrange(pattern, m=P))
             return raw
 
-        def load_yh(g):
-            b, i0 = divmod(g * G_ROWS, RES)
-            raw = raws.tile([P, BLOCKS, C], BF16, name="yh_raw", tag="yh_raw", bufs=5, align_bytes=64)
-            src = y_h[b * RES : (b + 1) * RES, i0 : i0 + G_ROWS, :]
-            nc.sync.dma_start(out=raw[:], in_=src.rearrange("j (ih il) c -> j ih il c", il=BLOCKS))
-            return raw
+        raw = {}
 
-        def load_x(g):
+        def load(k, g):
             b, i0 = divmod(g * G_ROWS, RES)
-            raw = raws.tile([P, BLOCKS, C], BF16, name="x_raw", tag="x_raw", bufs=5, align_bytes=64)
-            src = x[b, i0 : i0 + G_ROWS]
-            nc.sync.dma_start(out=raw[:], in_=src.rearrange("i (jh jl) c -> (i jh) jl c", jl=BLOCKS))
-            return raw
-
-        def load_yw(g):
-            raw = raws.tile([P, BLOCKS, C], U8, name="yw_raw", tag="yw_raw", bufs=5, align_bytes=64)
-            src = y_w_bytes[g * G_ROWS : (g + 1) * G_ROWS]
-            nc.sync.dma_start(out=raw[:], in_=src.rearrange("i (jh jl) c -> (i jh) jl c", jl=BLOCKS))
-            return raw
+            t = raws.tile([P, BLOCKS, C], U8 if k == "w" else BF16, name="raw_" + k, tag="raw_" + k, bufs=5, align_bytes=64)
+            if k == "h":
+                src = y_h[b * RES : (b + 1) * RES, i0 : i0 + G_ROWS, :].rearrange("j (ih il) c -> j ih il c", il=BLOCKS)
+            elif k == "x":
+                src = x[b, i0 : i0 + G_ROWS].rearrange("i (jh jl) c -> (i jh) jl c", jl=BLOCKS)
+            else:
+                src = y_w_bytes[g * G_ROWS : (g + 1) * G_ROWS].rearrange("i (jh jl) c -> (i jh) jl c", jl=BLOCKS)
+            nc.sync.dma_start(out=t[:], in_=src)
+            raw[k, g] = t
 
         logits = const.tile([P, IMAGES, 16], BF16, name="logits")
         nc.scalar.dma_start(out=logits[:, :, : 4 * BRANCHES], in_=a_logits.rearrange("b (p q) -> p b q", p=P))
@@ -83,21 +80,29 @@ def tile_dynamixerblock_pb_kernel(
         nc.scalar.dma_start(out=bias_h[:], in_=bo_h.rearrange("(p t) -> p t", p=P))
         bias_w = const.tile([P, BLOCKS], BF16, name="bias_w")
         nc.scalar.dma_start(out=bias_w[:], in_=bo_w.rearrange("(p t) -> p t", p=P))
-
-        wh_raw = load_weight(Wo_h, "(m t) k -> m t k", "wh_raw")
-        yh_raw = {0: load_yh(0)}
-        scale = const.tile([P, BLOCKS, C], F32, name="scale")
-        nc.sync.dma_start(out=scale[:, 0, :], in_=y_w_scale.rearrange("a o k -> (a o k)").partition_broadcast(P))
-        yw_raw = {0: load_yw(0)}
-        ww_raw = load_weight(Wo_w, "(m t) k -> m t k", "ww_raw")
-        x_raw = {0: load_x(0)}
-        wc_raw = load_weight(Wmlpc, "(m t) k -> m t k", "wc_raw")
-        yh_raw[1], x_raw[1], yw_raw[1] = load_yh(1), load_x(1), load_yw(1)
+        if MODE == "i":
+            scale = const.tile([P, BLOCKS], F32, name="scale")
+            nc.scalar.dma_start(out=scale[:], in_=y_w_scale.rearrange("a o (p t) -> p (a o t)", t=BLOCKS))
+        else:
+            scale = const.tile([P, C], F32, name="scale")
+        wraw = {}
+        wraw["h"] = load_weight(Wo_h, "(m t) k -> m t k", "wh_raw")
+        load("h", 0)
+        if MODE != "i":
+            nc.sync.dma_start(out=scale[:], in_=y_w_scale.rearrange("a o k -> (a o k)").partition_broadcast(P))
+        load("w", 0)
+        wraw["c"] = load_weight(Wmlpc, "(m t) k -> m t k", "wc_raw")
+        load("x", 0)
+        wraw["w"] = load_weight(Wo_w, "(m t) k -> m t k", "ww_raw")
+        for k in "hxw":
+            load(k, 1)
         bp_all = const.tile([P, C], BF16, name="bp_all")
         nc.sync.dma_start(out=bp_all[:], in_=bp.partition_broadcast(P))
-        wp_raw = load_weight(Wp, "(t m) k -> m t k", "wp_raw")
+        wraw["p"] = load_weight(Wp, "(t m) k -> m t k", "wp_raw")
+        for g in range(2, 5):
+            for k in "hxw":
+                load(k, g)
 
-        wide_all = {}
         lg = logits[:, :, : 4 * BRANCHES].rearrange("p b (t k) -> p b t k", k=BRANCHES)
         top = const.tile([P, IMAGES, BLOCKS], F32, name="top")
         nc.vector.tensor_reduce(out=top[:], in_=lg, axis=AX.X, op=ALU.max)
@@ -119,197 +124,163 @@ def tile_dynamixerblock_pb_kernel(
             nc.vector.tensor_tensor(out=bias[:, b], in0=a[:, 0, b], in1=bias_h[:], op=ALU.mult)
             nc.vector.tensor_tensor(out=bias_t[:, b], in0=a[:, 1, b], in1=bias_w[:], op=ALU.mult)
         nc.vector.tensor_tensor(out=bias[:], in0=bias[:], in1=bias_t[:], op=ALU.add)
-        for q in range(1, BLOCKS):
-            nc.vector.tensor_copy(out=scale[:, q, :], in_=scale[:, 0, :])
 
-        def turn_half(raw, idn, grouped, half):
-            words = raw[:].rearrange("p q c -> p (q c)").bitcast(F32)
-            pairs = grouped[:].bitcast(F32)
-            tr = ps_t.tile([P, 2, 2, P], F32, name="tr", tag="tr")
+        grp, trs, ops, wq, wide, sums, part, fs, fq, pss, res = {}, {}, {}, {}, {}, {}, {}, {}, {}, {}, {}
+        whole = slice(0, GROUP)
+
+        def get(table, key, make):
+            if key not in table:
+                table[key] = make()
+            return table[key]
+
+        def tile(shape, dtype, name, bufs=RING):
+            return work.tile(shape, dtype, name=name, tag=name, bufs=bufs, align_bytes=64)
+
+        def turn(src, idn, key, grouped, half):
+            words = src[:].rearrange("p q c -> p (q c)").bitcast(F32)
+            tr = ps_t.tile([P, 2, 2 * P], F32, name="tr", tag="tr")
             for q2 in range(2):
                 q = 2 * half + q2
                 for u in range(2):
-                    nc.tensor.transpose(tr[:, q2, u, :], words[:, 256 * q + u : 256 * (q + 1) : 2], idn[:])
-            return tr, pairs[:, 512 * half : 512 * (half + 1)]
+                    nc.tensor.transpose(tr[:, u, P * q2 : P * (q2 + 1)], words[:, 256 * q + u : 256 * (q + 1) : 2], idn[:])
+            trs[key] = (tr, grouped[:, 1024 * half : 1024 * (half + 1)])
 
-        def turn_out(tr, dst, eng):
-            o = dst.rearrange("p (q r u) -> p q r u", q=2, u=2)
-            i = tr[:].rearrange("p q u r -> p q r u")
+        def turn_out(key, eng):
+            tr, dst = trs[key]
+            if eng == "y":
+                nc.vector.tensor_tensor(
+                    out=dst.rearrange("p (n u e) -> p n u e", u=2, e=2),
+                    in0=tr[:].bitcast(BF16).rearrange("p u (n e) -> p n u e", e=2),
+                    in1=scale[:].rearrange("p (u e) -> p u e", e=2).unsqueeze(1).to_broadcast([P, 2 * P, 2, 2]),
+                    op=ALU.mult,
+                )
+                return
+            o = dst.bitcast(F32).rearrange("p (n u) -> p n u", u=2)
+            i = tr[:].rearrange("p u n -> p n u")
             if eng == "s":
                 nc.scalar.copy(out=o, in_=i)
             else:
                 nc.vector.tensor_copy(out=o, in_=i)
 
-        def turn_pe(raw, idn, name, bufs):
-            grouped = work.tile([P, GROUP * 4], BF16, name=name + "_g", tag=name + "_g", bufs=bufs, align_bytes=64)
-            return grouped, [turn_half(raw, idn, grouped, h) for h in range(2)]
-
-        def turn(raw, idn, name, bufs, engs="ss"):
-            grouped, parts = turn_pe(raw, idn, name, bufs)
-            for (tr, dst), e in zip(parts, engs):
-                turn_out(tr, dst, e)
-            return grouped
-
-        def quantize(grouped, name, pool, bufs):
+        def quantize(src, pool, name, bufs, width=GROUP):
             codes = pool.tile([P, GROUP], U32, name=name + "_c", tag=name + "_c", bufs=bufs, align_bytes=64)
             scales = pool.tile([P, GROUP], U8, name=name + "_s", tag=name + "_s", bufs=bufs, align_bytes=64)
-            nc.vector.quantize_mx(out=codes[:].bitcast(FP8X4), scales=scales[:], in_=grouped[:])
+            if src is not None:
+                nc.vector.quantize_mx(out=codes[:].bitcast(FP8X4), scales=scales[:], in_=src[:])
             return codes, scales
 
-        def widen(raw, wide, q):
-            nc.vector.tensor_tensor(out=wide[:, q : q + 1], in0=raw[:, q : q + 1].bitcast(FP8), in1=scale[:, q : q + 1], op=ALU.mult)
-
-        def mm(ps, st, sc, mv, mc):
+        def mm(ps, st, sc, mv):
             nc.tensor.matmul_mx(
-                out=ps,
-                lhsT=st[0][:, sc].bitcast(FP8X4),
-                lhsT_scale=st[1][:, sc],
-                rhs=mv[0][:, mc].bitcast(FP8X4),
-                rhs_scale=mv[1][:, mc],
-                start=True,
-                stop=True,
+                out=ps, lhsT=st[0][:, sc].bitcast(FP8X4), lhsT_scale=st[1][:, sc],
+                rhs=mv[0][:].bitcast(FP8X4), rhs_scale=mv[1][:], start=True, stop=True,
             )
 
-        whole = slice(0, GROUP)
-
-        def first_pe(g, t, ops):
-            sc = slice(P * t, P * (t + 1))
-            ph = ps_1.tile([P, GROUP], F32, name="ph", tag="m1")
-            mm(ph[:], wh, sc, ops["yh"], whole)
-            pc = ps_1.tile([P, GROUP], F32, name="pc", tag="m1")
-            mm(pc[:], wc, sc, ops["x"], whole)
-            pw = ps_1.tile([P, GROUP], F32, name="pw", tag="m1")
-            mm(pw[:], ww, sc, ops["yw"], whole)
-            return ph, pc, pw
-
-        def first_s(g, t, ps, sums, part):
+        def emit(tok, g):
+            op = tok[0]
             b = g * G_ROWS // RES
-            ph, pc, pw = ps
-            nc.scalar.activation(
-                out=sums[:, t, :].rearrange("p (ji il jh) -> p ji il jh", ji=16, il=4),
-                in_=ph[:].rearrange("p (il ji jh) -> p ji il jh", il=4, ji=16),
-                func=ACT.Identity,
-                scale=a[:, 0, b, t : t + 1],
-                bias=bias[:, b, t : t + 1],
-            )
-            nc.scalar.activation(out=part[:, t, :], in_=pw[:], func=ACT.Identity, scale=a[:, 1, b, t : t + 1], bias=0.0)
+            if op == "C":
+                wd = get(wide, g, lambda: tile([P, BLOCKS, C], BF16, "wide"))
+                h = int(tok[1])
+                if MODE == "i":
+                    nc.scalar.copy(out=wd[:, 2 * h : 2 * h + 2], in_=raw["w", g][:, 2 * h : 2 * h + 2].bitcast(FP8))
+                else:
+                    nc.vector.tensor_tensor(out=wd[:, h], in0=raw["w", g][:, h].bitcast(FP8), in1=scale[:], op=ALU.mult)
+            elif op == "T":
+                k, h = tok[1], int(tok[2])
+                gr = get(grp, (k, g), lambda: tile([P, GROUP * 4], BF16, "g_" + k))
+                turn(wide[g] if k == "w" else raw[k, g], ident_h if k == "h" else ident, (k, h, g), gr, h)
+                turned[g] = turned.get(g, 0) + 1
+                if turned[g] == 6 and g + 5 < GROUPS:
+                    for kk in "hxw":
+                        load(kk, g + 5)
+            elif op == "t":
+                k, h = tok[1], int(tok[2])
+                gr = get(grp, ("W", k), lambda: tile([P, GROUP * 4], BF16, "g_W", 2))
+                turn(wraw[k], ident, ("W", k, h), gr, h)
+            elif op == "E":
+                k, h = tok[1], int(tok[2])
+                turn_out((k, h, g), "y" if MODE == "i" and k == "w" else "v" if tok in ON_V else "s")
+            elif op == "e":
+                turn_out(("W", tok[1], int(tok[2])), "v" if tok in ON_V else "s")
+            elif op == "Q":
+                ops[tok[1], g] = quantize(grp[tok[1], g], work, "q_" + tok[1], RING)
+            elif op == "q":
+                wq[tok[1]] = quantize(grp["W", tok[1]], const, "wq_" + tok[1], 1)
+            elif op == "M":
+                k, t = tok[1], int(tok[2])
+                ps = ps_1.tile([P, GROUP], F32, name="m1", tag="m1")
+                mm(ps[:], wq[k], slice(P * t, P * (t + 1)), ops["x" if k == "c" else k, g])
+                pss[k, t, g] = ps
+            elif op == "A":
+                k, t = tok[1], int(tok[2])
+                ps = pss[k, t, g]
+                if k == "h":
+                    sm = get(sums, g, lambda: tile([P, BLOCKS, GROUP], F32, "sums"))
+                    nc.scalar.activation(
+                        out=sm[:, t, :].rearrange("p (ji il jh) -> p ji il jh", ji=16, il=4),
+                        in_=ps[:].rearrange("p (il ji jh) -> p ji il jh", il=4, ji=16),
+                        func=ACT.Identity, scale=a[:, 0, b, t : t + 1], bias=bias[:, b, t : t + 1],
+                    )
+                else:
+                    pt = get(part, g, lambda: tile([P, BLOCKS, GROUP], F32, "part"))
+                    nc.scalar.activation(out=pt[:, t, :], in_=ps[:], func=ACT.Copy, scale=a[:, 1, b, t : t + 1])
+            elif op == "S":
+                t = int(tok[2])
+                sm = sums[g]
+                nc.vector.scalar_tensor_tensor(
+                    out=sm[:, t, :], in0=pss["c", t, g][:], scalar=a[:, 2, b, t : t + 1], in1=sm[:, t, :], op0=ALU.mult, op1=ALU.add
+                )
+            elif op == "B":
+                f = get(fs, g, lambda: tile([P, GROUP * 4], BF16, "f"))
+                j = int(tok[1])
+                w = GROUP // NB
+                cols = slice(w * j, w * (j + 1))
+                (nc.vector if g == GROUPS - 1 and TAIL_V else nc.gpsimd).tensor_tensor(
+                    out=f[:, 4 * w * j : 4 * w * (j + 1)].rearrange("p (c i t) -> p c t i", i=4, t=4),
+                    in0=sums[g][:, :, cols].rearrange("p t (c i) -> p c t i", i=4),
+                    in1=part[g][:, :, cols].rearrange("p t (c i) -> p c t i", i=4),
+                    op=ALU.add,
+                )
+            elif op == "F":
+                j = int(tok[1])
+                codes, scales = get(fq, g, lambda: quantize(None, work, "q_f", RING))
+                w = GROUP // NF
+                cols = slice(w * j, w * (j + 1))
+                nc.vector.quantize_mx(out=codes[:, cols].bitcast(FP8X4), scales=scales[:, cols], in_=fs[g][:, 4 * w * j : 4 * w * (j + 1)])
+            elif op == "N":
+                q = int(tok[1])
+                ps = ps_2.tile([P, C], F32, name="m2", tag="m2")
+                mm(ps[:], fq[g], slice(P * q, P * (q + 1)), wq["p"])
+                pss["o", q, g] = ps
+            elif op in "OU":
+                q = int(tok[1])
+                rs = get(res, g, lambda: tile([P, BLOCKS, C], F32, "res"))
+                on_g = ("U%d" % q) + "@" in STEPS
+                if op == "O" and on_g:
+                    pl = tile([P, C], F32, "plain")
+                    nc.scalar.copy(out=pl[:], in_=pss["o", q, g][:])
+                    pss["u", q, g] = pl
+                    return
+                if op == "O":
+                    nc.vector.tensor_tensor(out=rs[:, q, :], in0=pss["o", q, g][:], in1=bp_all[:], op=ALU.add)
+                else:
+                    nc.gpsimd.tensor_tensor(out=rs[:, q, :], in0=pss["u", q, g][:], in1=bp_all[:], op=ALU.add)
+                stored[g] = stored.get(g, []) + [q]
+                i0 = g * G_ROWS % RES
+                dst = out[b, i0 : i0 + G_ROWS].rearrange("i (jh jl) c -> (i jh) jl c", jl=BLOCKS)
+                if g == GROUPS - 1:
+                    nc.sync.dma_start(out=dst[:, q : q + 1], in_=rs[:, q : q + 1])
+                elif len(stored[g]) == BLOCKS:
+                    nc.sync.dma_start(out=dst, in_=rs[:])
 
-        def first_v(g, t, ps, sums):
-            b = g * G_ROWS // RES
-            nc.vector.scalar_tensor_tensor(
-                out=sums[:, t, :], in0=ps[1][:], scalar=a[:, 2, b, t : t + 1], in1=sums[:, t, :], op0=ALU.mult, op1=ALU.add
-            )
-
-        def blend_half(eng, f, sums, part, h):
-            cols = slice(128 * h, 128 * (h + 1))
-            eng.tensor_tensor(
-                out=f[:, 512 * h : 512 * (h + 1)].rearrange("p (n t) -> p n t", t=4),
-                in0=sums[:, :, cols].rearrange("p t n -> p n t"),
-                in1=part[:, :, cols].rearrange("p t n -> p n t"),
-                op=ALU.add,
-            )
-
-        def second_pe(q, fq):
-            po = ps_2.tile([P, C], F32, name="po", tag="m2")
-            mm(po[:], fq, slice(P * q, P * (q + 1)), wpq, whole)
-            return po
-
-        def second_v(po, q, res):
-            nc.vector.tensor_tensor(out=res[:, q, :], in0=po[:], in1=bp_all[:], op=ALU.add)
-
-        def second_sg(po, q, res):
-            raw = work.tile([P, C], F32, name="plain", tag="plain", bufs=2, align_bytes=64)
-            nc.scalar.copy(out=raw[:], in_=po[:])
-            nc.gpsimd.tensor_tensor(out=res[:, q, :], in0=raw[:], in1=bp_all[:], op=ALU.add)
-
-        def store(g, res, q0, q1):
-            b, i0 = divmod(g * G_ROWS, RES)
-            dst = out[b, i0 : i0 + G_ROWS].rearrange("i (jh jl) c -> (i jh) jl c", jl=BLOCKS)
-            nc.sync.dma_start(out=dst[:, q0:q1], in_=res[:, q0:q1])
-
-        def wide_tile():
-            return work.tile([P, BLOCKS, C], BF16, name="wide", tag="wide", bufs=2, align_bytes=64)
-
-        NAMES = ("yh", "x", "yw")
-        srcs = {"yh": (yh_raw, ident_h), "x": (x_raw, ident), "yw": (wide_all, ident)}
-
-        def fetch(n):
-            yh_raw[n], x_raw[n], yw_raw[n] = load_yh(n), load_x(n), load_yw(n)
-
-        for n in range(2, 5):
-            fetch(n)
-
-        wh_g = turn(wh_raw, ident, "w", 2, HEADE[0:2])
-        yh_g = turn(yh_raw[0], ident_h, "yh", 2, HEADE[2:4])
-        wh = quantize(wh_g, "wh", const, 1)
-        wide_all[0] = wide_tile()
-        ops = {0: {"yh": quantize(yh_g, "yh", work, 2)}}
-        x_g = turn(x_raw[0], ident, "x", 2, HEADE[4:6])
-        for q in range(BLOCKS):
-            widen(yw_raw[0], wide_all[0], q)
-        wc_g = turn(wc_raw, ident, "w", 2, HEADE[6:8])
-        ops[0]["x"] = quantize(x_g, "x", work, 2)
-        wc = quantize(wc_g, "wc", const, 1)
-        yw_g = turn(wide_all[0], ident, "yw", 2, HEADE[8:10])
-        ww_g = turn(ww_raw, ident, "w", 2, HEADE[10:12])
-        ops[0]["yw"] = quantize(yw_g, "yw", work, 2)
-        ww = quantize(ww_g, "ww", const, 1)
-        wide_all[1] = wide_tile()
-        for q in range(BLOCKS):
-            widen(yw_raw[1], wide_all[1], q)
-
-        fq, summed, fs, ress, pos, trs, gro, pss = {}, {}, {}, {}, {}, {}, {}, {}
-        last = GROUPS - 1
-        for g in range(GROUPS + LAG):
-            for tok in (STEPS if g < GROUPS else TAIL).split():
-                op, arg = tok[0], tok[1:]
-                i = int(arg[0]) if arg else 0
-                if op == "L" and g + 5 < GROUPS:
-                    fetch(g + 5)
-                if op in "MAS" and g < GROUPS:
-                    if g not in summed:
-                        sums = work.tile([P, BLOCKS, GROUP], F32, name="sums", tag="sums", bufs=2, align_bytes=64)
-                        part = work.tile([P, BLOCKS, GROUP], F32, name="part", tag="part", bufs=2, align_bytes=64)
-                        summed[g] = (sums, part)
-                    if op == "M":
-                        pss[i] = first_pe(g, i, ops[g])
-                    elif op == "A":
-                        first_s(g, i, pss[i], *summed[g])
-                    else:
-                        first_v(g, i, pss[i], summed[g][0])
-                if op in "TEVQ" and g + 1 < GROUPS:
-                    nm = NAMES[i]
-                    if op == "T":
-                        h = int(arg[1])
-                        if h == 0:
-                            gro[nm] = work.tile([P, GROUP * 4], BF16, name=nm + "_g", tag=nm + "_g", bufs=2, align_bytes=64)
-                        trs[arg] = turn_half(srcs[nm][0][g + 1], srcs[nm][1], gro[nm], h)
-                    elif op == "E":
-                        turn_out(*trs[arg], "s")
-                    elif op == "V":
-                        turn_out(*trs[arg], "v")
-                    else:
-                        ops.setdefault(g + 1, {})[nm] = quantize(gro[nm], nm, work, 2)
-                if op == "P" and g == 0:
-                    wp_g = turn(wp_raw, ident, "w", 2)
-                    wpq = quantize(wp_g, "wpq", const, 1)
-                if op == "W" and g + 2 < GROUPS:
-                    if i == 0:
-                        wide_all[g + 2] = wide_tile()
-                    widen(yw_raw[g + 2], wide_all[g + 2], i)
-                if op in "BD" and 0 <= g - 1 < GROUPS:
-                    if g - 1 not in fs:
-                        fs[g - 1] = work.tile([P, GROUP * 4], BF16, name="f", tag="f", bufs=2, align_bytes=64)
-                    blend_half(nc.gpsimd if op == "B" else nc.vector, fs[g - 1], *summed[g - 1], i)
-                if op == "F" and 0 <= g - 1 < GROUPS:
-                    fq[g - 1] = quantize(fs[g - 1], "f", work, 2)
-                n = g - LAG
-                if op in "NOUX" and 0 <= n:
-                    if op == "N":
-                        pos[i] = second_pe(i, fq[n])
-                    elif op == "X":
-                        store(n, ress[n], int(arg[0]), int(arg[1]))
-                    else:
-                        if n not in ress:
-                            ress[n] = work.tile([P, BLOCKS, C], F32, name="res", tag="res", bufs=2, align_bytes=64)
-                        (second_v if op == "O" else second_sg)(pos[i], i, ress[n])
+        turned, stored = {}, {}
+        steps = [s.split("@") for s in STEPS.split()]
+        depth = max(int(lag) for tok, lag in steps)
+        for k in range(GROUPS + depth):
+            for tok, lag in steps:
+                g = k - int(lag)
+                if tok[0] in "teq":
+                    if g == 0:
+                        emit(tok, 0)
+                elif 0 <= g < GROUPS:
+                    emit(tok, g)

@@ -19,17 +19,19 @@ IMAGES = 4
 RES = 32
 BRANCHES = 3
 BLOCKS = 4
-G_ROWS = 16
-GROUP = G_ROWS * RES
-GROUPS = IMAGES * RES * RES // GROUP
+GROUP = 512
+ROWS = (8, 8, 16, 16, 16, 16, 16, 16, 8, 8)
+FIRST = [sum(ROWS[:g]) for g in range(len(ROWS))]
+GROUPS = len(ROWS)
 
-MODE = "i"
+MODE = "ii"
 TAIL_V = True
 RING = 2
 NB = 4
 NF = 2
-ON_V = "eh0 eh1 ec0 ec1 ew0 ew1 ep0 ep1".split()
-STEPS = "C0@0 th1@0 Ah2@2 th0@0 C1@0 Sc2@2 eh0@0 tc0@0 Ah0@1 ep0@2 Th0@0 eh1@0 Sc3@2 Eh0@0 qh@0 Mw1@2 Aw1@2 qp@3 Mw2@2 ec0@0 Aw2@2 F1@3 Th1@0 Eh1@0 F0@3 Tx0@0 Qw@1 Mw3@2 tw1@0 Qx@1 N0@3 Aw3@2 tw0@0 ew1@0 O3@4 Ex0@0 Mh1@1 ew0@0 Qh@0 B3@2 Mw0@1 Ah1@1 O0@3 qw@0 Aw0@1 Mc1@1 N1@3 tp1@2 Tx1@0 O1@3 ep1@2 Sc1@1 Mh3@1 B1@2 Ex1@0 tc1@0 Mc0@1 Ah3@1 ec1@0 Tw0@0 Sc0@1 N2@3 Ew0@0 Tw1@0 Mh2@1 Ew1@0 O2@3 N3@3 qc@0 Mc2@1 B2@2 Mh0@0 B0@2 Mc3@1 tp0@1"
+ON_V = "".split()
+STEPS = "th1@0 th0@0 eh1@0 Th0@0 eh0@0 tp1@2 Eh0@0 qh@0 tc1@0 Mw2@2 C0@0 tc0@0 ec1@0 O1@4 Aw2@2 qp@3 ec0@0 O0@4 ep1@2 qc@0 Sc0@2 Sc1@2 Qh@1 Mh1@1 Sc2@2 O2@4 Mh0@1 Ah1@1 Sc3@2 Ah0@1 Mh2@1 O3@4 Mw3@2 Qx@1 Tx0@0 Aw3@2 F0@3 Ah2@1 Th1@0 tw0@0 Qw@1 B1@2 N1@3 Ex0@0 B0@2 F1@3 qw@1 Eh1@0 ew0@0 Mw0@1 B2@2 Aw0@1 N0@3 B3@2 Mc0@1 Mh3@1 Mc1@1 Tx1@0 Ex1@0 Tw0@0 Mc2@1 Ah3@1 tw1@0 Ew0@0 tp0@1 N2@3 ep0@1 ew1@0 N3@3 Mc3@1 Tw1@0 Mw1@1 Ew1@0 Aw1@1"
+FULL_ONLY = "Th1 Tx1 Tw1 Eh1 Ex1 Ew1 C1 F1 N2 N3 O2 O3 U2 U3".split() + ["B%d" % j for j in range(NB // 2, NB)]
 
 FLOPS = 4 * 2 * (IMAGES * RES * RES) * C * C
 
@@ -49,11 +51,14 @@ def tile_dynamixerblock_pb_kernel(
 
         ident = const.tile([P, P], F32, name="ident")
         make_identity(nc, ident[:])
-        ident_h = const.tile([P, P], F32, name="ident_h")
-        nc.vector.tensor_copy(
-            out=ident_h[:].rearrange("p (jl ih jh) -> p jl ih jh", jl=4, ih=4, jh=8),
-            in_=ident[:].rearrange("p (jh jl ih) -> p jl ih jh", jl=4, ih=4, jh=8),
-        )
+        ident_h = {}
+        for rows in (8, 16):
+            il = rows // 4
+            ident_h[rows] = const.tile([P, P], F32, name="ident_h%d" % rows)
+            nc.vector.tensor_copy(
+                out=ident_h[rows][:].rearrange("p (jl ih jh) -> p jl ih jh", jl=il, ih=4),
+                in_=ident[:].rearrange("p (jh jl ih) -> p jl ih jh", jl=il, ih=4),
+            )
 
         def load_weight(w, pattern, name):
             raw = raws.tile([P, BLOCKS, C], BF16, name=name, tag="wraw", bufs=4, align_bytes=64)
@@ -63,15 +68,16 @@ def tile_dynamixerblock_pb_kernel(
         raw = {}
 
         def load(k, g):
-            b, i0 = divmod(g * G_ROWS, RES)
+            b, i0 = divmod(FIRST[g], RES)
+            rows, nb = ROWS[g], ROWS[g] // 4
             t = raws.tile([P, BLOCKS, C], U8 if k == "w" else BF16, name="raw_" + k, tag="raw_" + k, bufs=5, align_bytes=64)
             if k == "h":
-                src = y_h[b * RES : (b + 1) * RES, i0 : i0 + G_ROWS, :].rearrange("j (ih il) c -> j ih il c", il=BLOCKS)
+                src = y_h[b * RES : (b + 1) * RES, i0 : i0 + rows, :].rearrange("j (ih il) c -> j ih il c", il=nb)
             elif k == "x":
-                src = x[b, i0 : i0 + G_ROWS].rearrange("i (jh jl) c -> (i jh) jl c", jl=BLOCKS)
+                src = x[b, i0 : i0 + rows].rearrange("i (jh jl) c -> (i jh) jl c", jl=nb)
             else:
-                src = y_w_bytes[g * G_ROWS : (g + 1) * G_ROWS].rearrange("i (jh jl) c -> (i jh) jl c", jl=BLOCKS)
-            nc.sync.dma_start(out=t[:], in_=src)
+                src = y_w_bytes[FIRST[g] : FIRST[g] + rows].rearrange("i (jh jl) c -> (i jh) jl c", jl=nb)
+            nc.sync.dma_start(out=t[:, :nb], in_=src)
             raw[k, g] = t
 
         logits = const.tile([P, IMAGES, 16], BF16, name="logits")
@@ -84,23 +90,24 @@ def tile_dynamixerblock_pb_kernel(
             scale = const.tile([P, BLOCKS], F32, name="scale")
             nc.scalar.dma_start(out=scale[:], in_=y_w_scale.rearrange("a o (p t) -> p (a o t)", t=BLOCKS))
         else:
-            scale = const.tile([P, C], F32, name="scale")
+            scale = const.tile([P, BLOCKS, C], F32, name="scale")
         wraw = {}
         wraw["h"] = load_weight(Wo_h, "(m t) k -> m t k", "wh_raw")
         load("h", 0)
         if MODE != "i":
-            nc.sync.dma_start(out=scale[:], in_=y_w_scale.rearrange("a o k -> (a o k)").partition_broadcast(P))
+            nc.sync.dma_start(out=scale[:, 0], in_=y_w_scale.rearrange("a o k -> (a o k)").partition_broadcast(P))
         load("w", 0)
         wraw["c"] = load_weight(Wmlpc, "(m t) k -> m t k", "wc_raw")
         load("x", 0)
         wraw["w"] = load_weight(Wo_w, "(m t) k -> m t k", "ww_raw")
-        for k in "hxw":
-            load(k, 1)
+        for g in (1, 2):
+            for k in "hwx":
+                load(k, g)
         bp_all = const.tile([P, C], BF16, name="bp_all")
         nc.sync.dma_start(out=bp_all[:], in_=bp.partition_broadcast(P))
         wraw["p"] = load_weight(Wp, "(t m) k -> m t k", "wp_raw")
-        for g in range(2, 5):
-            for k in "hxw":
+        for g in (3, 4):
+            for k in "hwx":
                 load(k, g)
 
         lg = logits[:, :, : 4 * BRANCHES].rearrange("p b (t k) -> p b t k", k=BRANCHES)
@@ -125,6 +132,9 @@ def tile_dynamixerblock_pb_kernel(
             nc.vector.tensor_tensor(out=bias_t[:, b], in0=a[:, 1, b], in1=bias_w[:], op=ALU.mult)
         nc.vector.tensor_tensor(out=bias[:], in0=bias[:], in1=bias_t[:], op=ALU.add)
 
+        if MODE != "i":
+            for q in range(1, BLOCKS):
+                nc.vector.tensor_copy(out=scale[:, q], in_=scale[:, 0])
         grp, trs, ops, wq, wide, sums, part, fs, fq, pss, res = {}, {}, {}, {}, {}, {}, {}, {}, {}, {}, {}
         whole = slice(0, GROUP)
 
@@ -166,32 +176,35 @@ def tile_dynamixerblock_pb_kernel(
             codes = pool.tile([P, GROUP], U32, name=name + "_c", tag=name + "_c", bufs=bufs, align_bytes=64)
             scales = pool.tile([P, GROUP], U8, name=name + "_s", tag=name + "_s", bufs=bufs, align_bytes=64)
             if src is not None:
-                nc.vector.quantize_mx(out=codes[:].bitcast(FP8X4), scales=scales[:], in_=src[:])
+                nc.vector.quantize_mx(out=codes[:, :width].bitcast(FP8X4), scales=scales[:, :width], in_=src[:, : 4 * width])
             return codes, scales
 
-        def mm(ps, st, sc, mv):
+        def mm(ps, st, sc, mv, n):
             nc.tensor.matmul_mx(
                 out=ps, lhsT=st[0][:, sc].bitcast(FP8X4), lhsT_scale=st[1][:, sc],
-                rhs=mv[0][:].bitcast(FP8X4), rhs_scale=mv[1][:], start=True, stop=True,
+                rhs=mv[0][:, :n].bitcast(FP8X4), rhs_scale=mv[1][:, :n], start=True, stop=True,
             )
 
         def emit(tok, g):
             op = tok[0]
-            b = g * G_ROWS // RES
+            b = FIRST[g] // RES
+            rows = ROWS[g]
+            n = rows * RES
             if op == "C":
                 wd = get(wide, g, lambda: tile([P, BLOCKS, C], BF16, "wide"))
                 h = int(tok[1])
                 if MODE == "i":
                     nc.scalar.copy(out=wd[:, 2 * h : 2 * h + 2], in_=raw["w", g][:, 2 * h : 2 * h + 2].bitcast(FP8))
                 else:
-                    nc.vector.tensor_tensor(out=wd[:, h], in0=raw["w", g][:, h].bitcast(FP8), in1=scale[:], op=ALU.mult)
+                    nq = rows // 4
+                    nc.vector.tensor_tensor(out=wd[:, :nq], in0=raw["w", g][:, :nq].bitcast(FP8), in1=scale[:, :nq], op=ALU.mult)
             elif op == "T":
                 k, h = tok[1], int(tok[2])
                 gr = get(grp, (k, g), lambda: tile([P, GROUP * 4], BF16, "g_" + k))
-                turn(wide[g] if k == "w" else raw[k, g], ident_h if k == "h" else ident, (k, h, g), gr, h)
+                turn(wide[g] if k == "w" else raw[k, g], ident_h[rows] if k == "h" else ident, (k, h, g), gr, h)
                 turned[g] = turned.get(g, 0) + 1
-                if turned[g] == 6 and g + 5 < GROUPS:
-                    for kk in "hxw":
+                if turned[g] == 3 * rows // 8 and g + 5 < GROUPS:
+                    for kk in "hwx":
                         load(kk, g + 5)
             elif op == "t":
                 k, h = tok[1], int(tok[2])
@@ -203,13 +216,13 @@ def tile_dynamixerblock_pb_kernel(
             elif op == "e":
                 turn_out(("W", tok[1], int(tok[2])), "v" if tok in ON_V else "s")
             elif op == "Q":
-                ops[tok[1], g] = quantize(grp[tok[1], g], work, "q_" + tok[1], RING)
+                ops[tok[1], g] = quantize(grp[tok[1], g], work, "q_" + tok[1], RING, n)
             elif op == "q":
                 wq[tok[1]] = quantize(grp["W", tok[1]], const, "wq_" + tok[1], 1)
             elif op == "M":
                 k, t = tok[1], int(tok[2])
                 ps = ps_1.tile([P, GROUP], F32, name="m1", tag="m1")
-                mm(ps[:], wq[k], slice(P * t, P * (t + 1)), ops["x" if k == "c" else k, g])
+                mm(ps[:, :n], wq[k], slice(P * t, P * (t + 1)), ops["x" if k == "c" else k, g], n)
                 pss[k, t, g] = ps
             elif op == "A":
                 k, t = tok[1], int(tok[2])
@@ -217,18 +230,18 @@ def tile_dynamixerblock_pb_kernel(
                 if k == "h":
                     sm = get(sums, g, lambda: tile([P, BLOCKS, GROUP], F32, "sums"))
                     nc.scalar.activation(
-                        out=sm[:, t, :].rearrange("p (ji il jh) -> p ji il jh", ji=16, il=4),
-                        in_=ps[:].rearrange("p (il ji jh) -> p ji il jh", il=4, ji=16),
+                        out=sm[:, t, :n].rearrange("p (ji il jh) -> p ji il jh", ji=rows, il=rows // 4),
+                        in_=ps[:, :n].rearrange("p (il ji jh) -> p ji il jh", il=rows // 4, ji=rows),
                         func=ACT.Identity, scale=a[:, 0, b, t : t + 1], bias=bias[:, b, t : t + 1],
                     )
                 else:
                     pt = get(part, g, lambda: tile([P, BLOCKS, GROUP], F32, "part"))
-                    nc.scalar.activation(out=pt[:, t, :], in_=ps[:], func=ACT.Copy, scale=a[:, 1, b, t : t + 1])
+                    nc.scalar.activation(out=pt[:, t, :n], in_=ps[:, :n], func=ACT.Copy, scale=a[:, 1, b, t : t + 1])
             elif op == "S":
                 t = int(tok[2])
                 sm = sums[g]
                 nc.vector.scalar_tensor_tensor(
-                    out=sm[:, t, :], in0=pss["c", t, g][:], scalar=a[:, 2, b, t : t + 1], in1=sm[:, t, :], op0=ALU.mult, op1=ALU.add
+                    out=sm[:, t, :n], in0=pss["c", t, g][:, :n], scalar=a[:, 2, b, t : t + 1], in1=sm[:, t, :n], op0=ALU.mult, op1=ALU.add
                 )
             elif op == "B":
                 f = get(fs, g, lambda: tile([P, GROUP * 4], BF16, "f"))
@@ -250,11 +263,11 @@ def tile_dynamixerblock_pb_kernel(
             elif op == "N":
                 q = int(tok[1])
                 ps = ps_2.tile([P, C], F32, name="m2", tag="m2")
-                mm(ps[:], fq[g], slice(P * q, P * (q + 1)), wq["p"])
+                mm(ps[:], fq[g], slice(P * q, P * (q + 1)), wq["p"], C)
                 pss["o", q, g] = ps
             elif op in "OU":
                 q = int(tok[1])
-                rs = get(res, g, lambda: tile([P, BLOCKS, C], F32, "res"))
+                rs = get(res, g, lambda: tile([P, BLOCKS, C], F32, "res", 3))
                 on_g = ("U%d" % q) + "@" in STEPS
                 if op == "O" and on_g:
                     pl = tile([P, C], F32, "plain")
@@ -266,12 +279,12 @@ def tile_dynamixerblock_pb_kernel(
                 else:
                     nc.gpsimd.tensor_tensor(out=rs[:, q, :], in0=pss["u", q, g][:], in1=bp_all[:], op=ALU.add)
                 stored[g] = stored.get(g, []) + [q]
-                i0 = g * G_ROWS % RES
-                dst = out[b, i0 : i0 + G_ROWS].rearrange("i (jh jl) c -> (i jh) jl c", jl=BLOCKS)
+                i0 = FIRST[g] % RES
+                dst = out[b, i0 : i0 + rows].rearrange("i (jh jl) c -> (i jh) jl c", jl=rows // 4)
                 if g == GROUPS - 1:
                     nc.sync.dma_start(out=dst[:, q : q + 1], in_=rs[:, q : q + 1])
-                elif len(stored[g]) == BLOCKS:
-                    nc.sync.dma_start(out=dst, in_=rs[:])
+                elif len(stored[g]) == rows // 4:
+                    nc.sync.dma_start(out=dst, in_=rs[:, : rows // 4])
 
         turned, stored = {}, {}
         steps = [s.split("@") for s in STEPS.split()]
@@ -282,5 +295,5 @@ def tile_dynamixerblock_pb_kernel(
                 if tok[0] in "teq":
                     if g == 0:
                         emit(tok, 0)
-                elif 0 <= g < GROUPS:
+                elif 0 <= g < GROUPS and (ROWS[g] == 16 or tok not in FULL_ONLY):
                     emit(tok, g)

from contextlib import ExitStack

import concourse.mybir as mybir
from concourse.masks import make_identity

F32 = mybir.dt.float32
BF16 = mybir.dt.bfloat16
U32 = mybir.dt.uint32
U8 = mybir.dt.uint8
FP8 = mybir.dt.float8_e4m3fn
FP8X4 = mybir.dt.float8_e4m3fn_x4
ALU = mybir.AluOpType
ACT = mybir.ActivationFunctionType
AX = mybir.AxisListType

P = 128
C = 512
IMAGES = 4
RES = 32
BRANCHES = 3
BLOCKS = 4
GROUP = 512
ROWS = (8, 8, 16, 16, 16, 16, 16, 16, 8, 8)
FIRST = [sum(ROWS[:g]) for g in range(len(ROWS))]
GROUPS = len(ROWS)

MODE = "ii"
TAIL_V = True
RING = 2
NB = 4
NF = 2
ON_V = "".split()
STEPS = "th1@0 th0@0 eh1@0 Th0@0 eh0@0 tp1@2 Eh0@0 qh@0 tc1@0 Mw2@2 C0@0 tc0@0 ec1@0 O1@4 Aw2@2 qp@3 ec0@0 O0@4 ep1@2 qc@0 Sc0@2 Sc1@2 Qh@1 Mh1@1 Sc2@2 O2@4 Mh0@1 Ah1@1 Sc3@2 Ah0@1 Mh2@1 O3@4 Mw3@2 Qx@1 Tx0@0 Aw3@2 F0@3 Ah2@1 Th1@0 tw0@0 Qw@1 B1@2 N1@3 Ex0@0 B0@2 F1@3 qw@1 Eh1@0 ew0@0 Mw0@1 B2@2 Aw0@1 N0@3 B3@2 Mc0@1 Mh3@1 Mc1@1 Tx1@0 Ex1@0 Tw0@0 Mc2@1 Ah3@1 tw1@0 Ew0@0 tp0@1 N2@3 ep0@1 ew1@0 N3@3 Mc3@1 Tw1@0 Mw1@1 Ew1@0 Aw1@1"
FULL_ONLY = "Th1 Tx1 Tw1 Eh1 Ex1 Ew1 C1 F1 N2 N3 O2 O3 U2 U3".split() + ["B%d" % j for j in range(NB // 2, NB)]

FLOPS = 4 * 2 * (IMAGES * RES * RES) * C * C


def tile_dynamixerblock_pb_kernel(
    tc, y_h, y_w_bytes, y_w_scale, x, a_logits, Wo_h, bo_h, Wo_w, bo_w, Wmlpc, Wp, bp, out
):
    nc = tc.nc
    with ExitStack() as ctx:
        const = ctx.enter_context(tc.tile_pool(name="const", bufs=1))
        raws = ctx.enter_context(tc.tile_pool(name="raws", bufs=3))
        work = ctx.enter_context(tc.tile_pool(name="work", bufs=2))
        ps_t = ctx.enter_context(tc.psum_pool(name="ps_t", bufs=2))
        ps_1 = ctx.enter_context(tc.psum_pool(name="ps_1", bufs=4))
        ps_2 = ctx.enter_context(tc.psum_pool(name="ps_2", bufs=2))
        ctx.enter_context(tc.manual_schedule())

        ident = const.tile([P, P], F32, name="ident")
        make_identity(nc, ident[:])
        ident_h = {}
        for rows in (8, 16):
            il = rows // 4
            ident_h[rows] = const.tile([P, P], F32, name="ident_h%d" % rows)
            nc.vector.tensor_copy(
                out=ident_h[rows][:].rearrange("p (jl ih jh) -> p jl ih jh", jl=il, ih=4),
                in_=ident[:].rearrange("p (jh jl ih) -> p jl ih jh", jl=il, ih=4),
            )

        def load_weight(w, pattern, name):
            raw = raws.tile([P, BLOCKS, C], BF16, name=name, tag="wraw", bufs=4, align_bytes=64)
            nc.sync.dma_start(out=raw[:], in_=w.rearrange(pattern, m=P))
            return raw

        raw = {}

        def load(k, g):
            b, i0 = divmod(FIRST[g], RES)
            rows, nb = ROWS[g], ROWS[g] // 4
            t = raws.tile([P, BLOCKS, C], U8 if k == "w" else BF16, name="raw_" + k, tag="raw_" + k, bufs=5, align_bytes=64)
            if k == "h":
                src = y_h[b * RES : (b + 1) * RES, i0 : i0 + rows, :].rearrange("j (ih il) c -> j ih il c", il=nb)
            elif k == "x":
                src = x[b, i0 : i0 + rows].rearrange("i (jh jl) c -> (i jh) jl c", jl=nb)
            else:
                src = y_w_bytes[FIRST[g] : FIRST[g] + rows].rearrange("i (jh jl) c -> (i jh) jl c", jl=nb)
            nc.sync.dma_start(out=t[:, :nb], in_=src)
            raw[k, g] = t

        logits = const.tile([P, IMAGES, 16], BF16, name="logits")
        nc.scalar.dma_start(out=logits[:, :, : 4 * BRANCHES], in_=a_logits.rearrange("b (p q) -> p b q", p=P))
        bias_h = const.tile([P, BLOCKS], BF16, name="bias_h")
        nc.scalar.dma_start(out=bias_h[:], in_=bo_h.rearrange("(p t) -> p t", p=P))
        bias_w = const.tile([P, BLOCKS], BF16, name="bias_w")
        nc.scalar.dma_start(out=bias_w[:], in_=bo_w.rearrange("(p t) -> p t", p=P))
        if MODE == "i":
            scale = const.tile([P, BLOCKS], F32, name="scale")
            nc.scalar.dma_start(out=scale[:], in_=y_w_scale.rearrange("a o (p t) -> p (a o t)", t=BLOCKS))
        else:
            scale = const.tile([P, BLOCKS, C], F32, name="scale")
        wraw = {}
        wraw["h"] = load_weight(Wo_h, "(m t) k -> m t k", "wh_raw")
        load("h", 0)
        if MODE != "i":
            nc.sync.dma_start(out=scale[:, 0], in_=y_w_scale.rearrange("a o k -> (a o k)").partition_broadcast(P))
        load("w", 0)
        wraw["c"] = load_weight(Wmlpc, "(m t) k -> m t k", "wc_raw")
        load("x", 0)
        wraw["w"] = load_weight(Wo_w, "(m t) k -> m t k", "ww_raw")
        for g in (1, 2):
            for k in "hwx":
                load(k, g)
        bp_all = const.tile([P, C], BF16, name="bp_all")
        nc.sync.dma_start(out=bp_all[:], in_=bp.partition_broadcast(P))
        wraw["p"] = load_weight(Wp, "(t m) k -> m t k", "wp_raw")
        for g in (3, 4):
            for k in "hwx":
                load(k, g)

        lg = logits[:, :, : 4 * BRANCHES].rearrange("p b (t k) -> p b t k", k=BRANCHES)
        top = const.tile([P, IMAGES, BLOCKS], F32, name="top")
        nc.vector.tensor_reduce(out=top[:], in_=lg, axis=AX.X, op=ALU.max)
        wts = const.tile([P, IMAGES, BLOCKS, BRANCHES], F32, name="wts")
        for k in range(BRANCHES):
            nc.vector.tensor_tensor(out=wts[:, :, :, k], in0=lg[:, :, :, k], in1=top[:], op=ALU.subtract)
        flat = wts[:].rearrange("p b t k -> p (b t k)")
        nc.scalar.activation(out=flat, in_=flat, func=ACT.Exp)
        total = const.tile([P, IMAGES, BLOCKS], F32, name="total")
        nc.vector.tensor_reduce(out=total[:], in_=wts[:], axis=AX.X, op=ALU.add)
        inv = const.tile([P, IMAGES, BLOCKS], F32, name="inv")
        nc.vector.reciprocal(out=inv[:], in_=total[:])
        a = const.tile([P, BRANCHES, IMAGES, BLOCKS], F32, name="a")
        for k in range(BRANCHES):
            nc.vector.tensor_tensor(out=a[:, k], in0=wts[:, :, :, k], in1=inv[:], op=ALU.mult)
        bias = const.tile([P, IMAGES, BLOCKS], F32, name="bias")
        bias_t = const.tile([P, IMAGES, BLOCKS], F32, name="bias_t")
        for b in range(IMAGES):
            nc.vector.tensor_tensor(out=bias[:, b], in0=a[:, 0, b], in1=bias_h[:], op=ALU.mult)
            nc.vector.tensor_tensor(out=bias_t[:, b], in0=a[:, 1, b], in1=bias_w[:], op=ALU.mult)
        nc.vector.tensor_tensor(out=bias[:], in0=bias[:], in1=bias_t[:], op=ALU.add)

        if MODE != "i":
            for q in range(1, BLOCKS):
                nc.vector.tensor_copy(out=scale[:, q], in_=scale[:, 0])
        grp, trs, ops, wq, wide, sums, part, fs, fq, pss, res = {}, {}, {}, {}, {}, {}, {}, {}, {}, {}, {}
        whole = slice(0, GROUP)

        def get(table, key, make):
            if key not in table:
                table[key] = make()
            return table[key]

        def tile(shape, dtype, name, bufs=RING):
            return work.tile(shape, dtype, name=name, tag=name, bufs=bufs, align_bytes=64)

        def turn(src, idn, key, grouped, half):
            words = src[:].rearrange("p q c -> p (q c)").bitcast(F32)
            tr = ps_t.tile([P, 2, 2 * P], F32, name="tr", tag="tr")
            for q2 in range(2):
                q = 2 * half + q2
                for u in range(2):
                    nc.tensor.transpose(tr[:, u, P * q2 : P * (q2 + 1)], words[:, 256 * q + u : 256 * (q + 1) : 2], idn[:])
            trs[key] = (tr, grouped[:, 1024 * half : 1024 * (half + 1)])

        def turn_out(key, eng):
            tr, dst = trs[key]
            if eng == "y":
                nc.vector.tensor_tensor(
                    out=dst.rearrange("p (n u e) -> p n u e", u=2, e=2),
                    in0=tr[:].bitcast(BF16).rearrange("p u (n e) -> p n u e", e=2),
                    in1=scale[:].rearrange("p (u e) -> p u e", e=2).unsqueeze(1).to_broadcast([P, 2 * P, 2, 2]),
                    op=ALU.mult,
                )
                return
            o = dst.bitcast(F32).rearrange("p (n u) -> p n u", u=2)
            i = tr[:].rearrange("p u n -> p n u")
            if eng == "s":
                nc.scalar.copy(out=o, in_=i)
            else:
                nc.vector.tensor_copy(out=o, in_=i)

        def quantize(src, pool, name, bufs, width=GROUP):
            codes = pool.tile([P, GROUP], U32, name=name + "_c", tag=name + "_c", bufs=bufs, align_bytes=64)
            scales = pool.tile([P, GROUP], U8, name=name + "_s", tag=name + "_s", bufs=bufs, align_bytes=64)
            if src is not None:
                nc.vector.quantize_mx(out=codes[:, :width].bitcast(FP8X4), scales=scales[:, :width], in_=src[:, : 4 * width])
            return codes, scales

        def mm(ps, st, sc, mv, n):
            nc.tensor.matmul_mx(
                out=ps, lhsT=st[0][:, sc].bitcast(FP8X4), lhsT_scale=st[1][:, sc],
                rhs=mv[0][:, :n].bitcast(FP8X4), rhs_scale=mv[1][:, :n], start=True, stop=True,
            )

        def emit(tok, g):
            op = tok[0]
            b = FIRST[g] // RES
            rows = ROWS[g]
            n = rows * RES
            if op == "C":
                wd = get(wide, g, lambda: tile([P, BLOCKS, C], BF16, "wide"))
                h = int(tok[1])
                if MODE == "i":
                    nc.scalar.copy(out=wd[:, 2 * h : 2 * h + 2], in_=raw["w", g][:, 2 * h : 2 * h + 2].bitcast(FP8))
                else:
                    nq = rows // 4
                    nc.vector.tensor_tensor(out=wd[:, :nq], in0=raw["w", g][:, :nq].bitcast(FP8), in1=scale[:, :nq], op=ALU.mult)
            elif op == "T":
                k, h = tok[1], int(tok[2])
                gr = get(grp, (k, g), lambda: tile([P, GROUP * 4], BF16, "g_" + k))
                turn(wide[g] if k == "w" else raw[k, g], ident_h[rows] if k == "h" else ident, (k, h, g), gr, h)
                turned[g] = turned.get(g, 0) + 1
                if turned[g] == 3 * rows // 8 and g + 5 < GROUPS:
                    for kk in "hwx":
                        load(kk, g + 5)
            elif op == "t":
                k, h = tok[1], int(tok[2])
                gr = get(grp, ("W", k), lambda: tile([P, GROUP * 4], BF16, "g_W", 2))
                turn(wraw[k], ident, ("W", k, h), gr, h)
            elif op == "E":
                k, h = tok[1], int(tok[2])
                turn_out((k, h, g), "y" if MODE == "i" and k == "w" else "v" if tok in ON_V else "s")
            elif op == "e":
                turn_out(("W", tok[1], int(tok[2])), "v" if tok in ON_V else "s")
            elif op == "Q":
                ops[tok[1], g] = quantize(grp[tok[1], g], work, "q_" + tok[1], RING, n)
            elif op == "q":
                wq[tok[1]] = quantize(grp["W", tok[1]], const, "wq_" + tok[1], 1)
            elif op == "M":
                k, t = tok[1], int(tok[2])
                ps = ps_1.tile([P, GROUP], F32, name="m1", tag="m1")
                mm(ps[:, :n], wq[k], slice(P * t, P * (t + 1)), ops["x" if k == "c" else k, g], n)
                pss[k, t, g] = ps
            elif op == "A":
                k, t = tok[1], int(tok[2])
                ps = pss[k, t, g]
                if k == "h":
                    sm = get(sums, g, lambda: tile([P, BLOCKS, GROUP], F32, "sums"))
                    nc.scalar.activation(
                        out=sm[:, t, :n].rearrange("p (ji il jh) -> p ji il jh", ji=rows, il=rows // 4),
                        in_=ps[:, :n].rearrange("p (il ji jh) -> p ji il jh", il=rows // 4, ji=rows),
                        func=ACT.Identity, scale=a[:, 0, b, t : t + 1], bias=bias[:, b, t : t + 1],
                    )
                else:
                    pt = get(part, g, lambda: tile([P, BLOCKS, GROUP], F32, "part"))
                    nc.scalar.activation(out=pt[:, t, :n], in_=ps[:, :n], func=ACT.Copy, scale=a[:, 1, b, t : t + 1])
            elif op == "S":
                t = int(tok[2])
                sm = sums[g]
                nc.vector.scalar_tensor_tensor(
                    out=sm[:, t, :n], in0=pss["c", t, g][:, :n], scalar=a[:, 2, b, t : t + 1], in1=sm[:, t, :n], op0=ALU.mult, op1=ALU.add
                )
            elif op == "B":
                f = get(fs, g, lambda: tile([P, GROUP * 4], BF16, "f"))
                j = int(tok[1])
                w = GROUP // NB
                cols = slice(w * j, w * (j + 1))
                (nc.vector if g == GROUPS - 1 and TAIL_V else nc.gpsimd).tensor_tensor(
                    out=f[:, 4 * w * j : 4 * w * (j + 1)].rearrange("p (c i t) -> p c t i", i=4, t=4),
                    in0=sums[g][:, :, cols].rearrange("p t (c i) -> p c t i", i=4),
                    in1=part[g][:, :, cols].rearrange("p t (c i) -> p c t i", i=4),
                    op=ALU.add,
                )
            elif op == "F":
                j = int(tok[1])
                codes, scales = get(fq, g, lambda: quantize(None, work, "q_f", RING))
                w = GROUP // NF
                cols = slice(w * j, w * (j + 1))
                nc.vector.quantize_mx(out=codes[:, cols].bitcast(FP8X4), scales=scales[:, cols], in_=fs[g][:, 4 * w * j : 4 * w * (j + 1)])
            elif op == "N":
                q = int(tok[1])
                ps = ps_2.tile([P, C], F32, name="m2", tag="m2")
                mm(ps[:], fq[g], slice(P * q, P * (q + 1)), wq["p"], C)
                pss["o", q, g] = ps
            elif op in "OU":
                q = int(tok[1])
                rs = get(res, g, lambda: tile([P, BLOCKS, C], F32, "res", 3))
                on_g = ("U%d" % q) + "@" in STEPS
                if op == "O" and on_g:
                    pl = tile([P, C], F32, "plain")
                    nc.scalar.copy(out=pl[:], in_=pss["o", q, g][:])
                    pss["u", q, g] = pl
                    return
                if op == "O":
                    nc.vector.tensor_tensor(out=rs[:, q, :], in0=pss["o", q, g][:], in1=bp_all[:], op=ALU.add)
                else:
                    nc.gpsimd.tensor_tensor(out=rs[:, q, :], in0=pss["u", q, g][:], in1=bp_all[:], op=ALU.add)
                stored[g] = stored.get(g, []) + [q]
                i0 = FIRST[g] % RES
                dst = out[b, i0 : i0 + rows].rearrange("i (jh jl) c -> (i jh) jl c", jl=rows // 4)
                if g == GROUPS - 1:
                    nc.sync.dma_start(out=dst[:, q : q + 1], in_=rs[:, q : q + 1])
                elif len(stored[g]) == rows // 4:
                    nc.sync.dma_start(out=dst, in_=rs[:, : rows // 4])

        turned, stored = {}, {}
        steps = [s.split("@") for s in STEPS.split()]
        depth = max(int(lag) for tok, lag in steps)
        for k in range(GROUPS + depth):
            for tok, lag in steps:
                g = k - int(lag)
                if tok[0] in "teq":
                    if g == 0:
                        emit(tok, 0)
                elif 0 <= g < GROUPS and (ROWS[g] == 16 or tok not in FULL_ONLY):
                    emit(tok, g)
